import numpy as np
import ml_dtypes

BF16 = ml_dtypes.bfloat16


def bf(x):
    return np.asarray(x, np.float32).astype(BF16)


def f32(x):
    return np.asarray(x, np.float32)


def f64(x):
    return np.asarray(x).astype(np.float64)


def striped(idx):
    return np.tile(idx.reshape(-1, 16).T, (8, 1))


H, D, T, S, N, C = 4, 128, 512, 2048, 512, 512


def setup_inputs():
    return {
        "base": f32(0.5 * np.random.standard_normal((C, S))),
        "q": bf(np.random.standard_normal((C, N))),
        "k": bf(np.random.standard_normal((C, T))),
        "v": bf(2.0 * np.random.standard_normal((T, C))),
        "adj": f32(np.random.uniform(size=(T, N))),
        "dist": f32(np.random.uniform(size=(T, N))),
        "wa": f32(np.repeat(0.5 + 0.5 * np.random.uniform(size=(H, 1)), D, axis=0)),
        "wd": f32(np.repeat(-0.5 - 0.5 * np.random.uniform(size=(H, 1)), D, axis=0)),
        "offs": striped(np.random.permutation(S)[:N]),
    }


def reference(base, q, k, v, adj, dist, wa, wd, offs):
    idx = offs[:16].T.reshape(-1)
    out = f64(base).copy()
    q3 = f64(q).reshape(H, D, N)
    k3 = f64(k).reshape(H, D, T)
    v3 = f64(v).reshape(T, H, D)
    for h in range(H):
        mod = 1.0 + f64(adj) * f64(wa)[h * D, 0] + f64(dist) * f64(wd)[h * D, 0]
        s = (k3[h].T @ q3[h]) * mod / np.sqrt(D)
        e = np.exp(s)
        u = v3[:, h].T @ e
        r = 1.0 / e.sum(axis=0, keepdims=True)
        out[h * D:(h + 1) * D, idx] = u * r
    return out

@@ -1,0 +1,101 @@
+import math
+
+import concourse.mybir as mybir
+from concourse.masks import make_identity
+
+H, D, T, S, N = 4, 128, 512, 2048, 512
+P = 128
+KEY_BLOCKS = T // P
+QUERY_BLOCKS = N // P
+FLOPS = 4 * H * D * T * N
+
+F32, BF16, U16 = mybir.dt.float32, mybir.dt.bfloat16, mybir.dt.uint16
+MULT, ADD = mybir.AluOpType.mult, mybir.AluOpType.add
+ACT = mybir.ActivationFunctionType
+
+
+def tile_msrsa_kernel(tc, base, q, k, v, adj, dist, wa, wd, offs, out):
+    nc = tc.nc
+    with (
+        tc.tile_pool(name="held", bufs=1) as held,
+        tc.tile_pool(name="work", bufs=3) as work,
+        tc.tile_pool(name="exps", bufs=2 * KEY_BLOCKS) as exps,
+        tc.tile_pool(name="tails", bufs=2) as tails,
+        tc.psum_pool(name="psum_s", bufs=3) as psum_s,
+        tc.psum_pool(name="psum_u", bufs=2) as psum_u,
+        tc.psum_pool(name="psum_z", bufs=1) as psum_z,
+        tc.psum_pool(name="psum_r", bufs=2) as psum_r,
+    ):
+        offsets = held.tile([P, N // 16], U16, name="offsets")
+        nc.sync.dma_start(offsets[:], offs)
+
+        wa_rows = held.tile([P, H * D], F32, name="wa_rows")
+        wd_rows = held.tile([P, H * D], F32, name="wd_rows")
+        nc.sync.dma_start(wa_rows[:], wa.rearrange("c o -> (c o)").partition_broadcast(P))
+        nc.sync.dma_start(wd_rows[:], wd.rearrange("c o -> (c o)").partition_broadcast(P))
+
+        q_head = [held.tile([P, N], BF16, name=f"q_head{h}") for h in range(H)]
+        k_head = [held.tile([P, T], BF16, name=f"k_head{h}") for h in range(H)]
+        window = [held.tile([P, S], F32, name=f"window{h}") for h in range(H)]
+        adj_block = [held.tile([P, N], F32, name=f"adj_block{b}") for b in range(KEY_BLOCKS)]
+        dist_block = [held.tile([P, N], F32, name=f"dist_block{b}") for b in range(KEY_BLOCKS)]
+        v_block = [held.tile([P, H * D], BF16, name=f"v_block{b}") for b in range(KEY_BLOCKS)]
+
+        def rows(dram, i):
+            return dram[i * P : (i + 1) * P, :]
+
+        nc.sync.dma_start(q_head[0][:], rows(q, 0))
+        nc.sync.dma_start(k_head[0][:], rows(k, 0))
+        for b in range(KEY_BLOCKS):
+            nc.sync.dma_start(adj_block[b][:], rows(adj, b))
+            nc.sync.dma_start(dist_block[b][:], rows(dist, b))
+            nc.sync.dma_start(v_block[b][:], rows(v, b))
+        nc.sync.dma_start(window[0][:], rows(base, 0))
+        for h in range(1, H):
+            nc.sync.dma_start(q_head[h][:], rows(q, h))
+            nc.sync.dma_start(k_head[h][:], rows(k, h))
+            nc.sync.dma_start(window[h][:], rows(base, h))
+
+        ones_column = held.tile([P, 1], BF16, name="ones_column")
+        nc.vector.memset(ones_column[:], 1.0)
+        identity = held.tile([P, P], F32, name="identity")
+        make_identity(nc, identity[:])
+
+        for h in range(H):
+            wa_h = wa_rows[:, h * D : h * D + 1]
+            wd_h = wd_rows[:, h * D : h * D + 1]
+
+            u_psum = psum_u.tile([P, N], F32, name="u_psum")
+            e_block = []
+            for b in range(KEY_BLOCKS):
+                s_psum = psum_s.tile([P, N], F32, name="s_psum")
+                nc.tensor.matmul(s_psum[:], lhsT=k_head[h][:, b * P : (b + 1) * P], rhs=q_head[h][:], start=True, stop=True)
+
+                adj_part = work.tile([P, N], F32, name="adj_part")
+                nc.scalar.activation(adj_part[:], adj_block[b][:], ACT.Identity, bias=1.0, scale=wa_h)
+                modulation = work.tile([P, N], F32, name="modulation")
+                nc.vector.scalar_tensor_tensor(modulation[:], dist_block[b][:], wd_h, adj_part[:], MULT, ADD)
+                modulated = work.tile([P, N], F32, name="modulated")
+                nc.vector.tensor_tensor(modulated[:], s_psum[:], modulation[:], MULT)
+
+                e = exps.tile([P, N], BF16, name="e")
+                nc.scalar.activation(e[:], modulated[:], ACT.Exp, scale=1.0 / math.sqrt(D))
+                e_block.append(e)
+                nc.tensor.matmul(u_psum[:], lhsT=v_block[b][:, h * D : (h + 1) * D], rhs=e[:], start=(b == 0), stop=(b == KEY_BLOCKS - 1))
+
+            sums_psum = psum_z.tile([P, QUERY_BLOCKS], F32, name="sums_psum")
+            for c in range(QUERY_BLOCKS):
+                for b in range(KEY_BLOCKS):
+                    nc.tensor.matmul(sums_psum[:, c : c + 1], lhsT=e_block[b][:, c * P : (c + 1) * P], rhs=ones_column[:], start=(b == 0), stop=(b == KEY_BLOCKS - 1))
+            r_columns = tails.tile([P, QUERY_BLOCKS], F32, name="r_columns")
+            nc.vector.reciprocal(r_columns[:], sums_psum[:])
+            r_psum = psum_r.tile([P, N], F32, name="r_psum")
+            for c in range(QUERY_BLOCKS):
+                nc.tensor.transpose(r_psum[:, c * P : (c + 1) * P], r_columns[:, c : c + 1].to_broadcast([P, P]), identity[:])
+
+            u = tails.tile([P, N], F32, name="u")
+            nc.scalar.copy(u[:], u_psum[:])
+            r = tails.tile([P, N], F32, name="r")
+            nc.scalar.copy(r[:], r_psum[:])
+            nc.vector.tensor_tensor(window[h][:].indirect(offsets[:]), u[:], r[:], MULT)
+            nc.sync.dma_start(rows(out, h), window[h][:])

@@ -7,11 +7,16 @@ H, D, T, S, N = 4, 128, 512, 2048, 512
 P = 128
 KEY_BLOCKS = T // P
 QUERY_BLOCKS = N // P
+BLOCKS = H * KEY_BLOCKS
 FLOPS = 4 * H * D * T * N
 
 F32, BF16, U16 = mybir.dt.float32, mybir.dt.bfloat16, mybir.dt.uint16
 MULT, ADD = mybir.AluOpType.mult, mybir.AluOpType.add
 ACT = mybir.ActivationFunctionType
+
+
+def rows(dram, i):
+    return dram[i * P : (i + 1) * P, :]
 
 
 def tile_msrsa_kernel(tc, base, q, k, v, adj, dist, wa, wd, offs, out):
@@ -29,10 +34,11 @@ def tile_msrsa_kernel(tc, base, q, k, v, adj, dist, wa, wd, offs, out):
         offsets = held.tile([P, N // 16], U16, name="offsets")
         nc.sync.dma_start(offsets[:], offs)
 
-        wa_rows = held.tile([P, H * D], F32, name="wa_rows")
-        wd_rows = held.tile([P, H * D], F32, name="wd_rows")
-        nc.sync.dma_start(wa_rows[:], wa.rearrange("c o -> (c o)").partition_broadcast(P))
-        nc.sync.dma_start(wd_rows[:], wd.rearrange("c o -> (c o)").partition_broadcast(P))
+        wa_heads = held.tile([P, H], F32, name="wa_heads")
+        wd_heads = held.tile([P, H], F32, name="wd_heads")
+        with nc.allow_non_contiguous_dma(reason="two loads of 512 single float32 values"):
+            nc.scalar.dma_start(wa_heads[:], wa.rearrange("(h d) o -> d (h o)", d=D))
+            nc.scalar.dma_start(wd_heads[:], wd.rearrange("(h d) o -> d (h o)", d=D))
 
         q_head = [held.tile([P, N], BF16, name=f"q_head{h}") for h in range(H)]
         k_head = [held.tile([P, T], BF16, name=f"k_head{h}") for h in range(H)]
@@ -41,61 +47,75 @@ def tile_msrsa_kernel(tc, base, q, k, v, adj, dist, wa, wd, offs, out):
         dist_block = [held.tile([P, N], F32, name=f"dist_block{b}") for b in range(KEY_BLOCKS)]
         v_block = [held.tile([P, H * D], BF16, name=f"v_block{b}") for b in range(KEY_BLOCKS)]
 
-        def rows(dram, i):
-            return dram[i * P : (i + 1) * P, :]
-
         nc.sync.dma_start(q_head[0][:], rows(q, 0))
         nc.sync.dma_start(k_head[0][:], rows(k, 0))
         for b in range(KEY_BLOCKS):
             nc.sync.dma_start(adj_block[b][:], rows(adj, b))
             nc.sync.dma_start(dist_block[b][:], rows(dist, b))
             nc.sync.dma_start(v_block[b][:], rows(v, b))
-        nc.sync.dma_start(window[0][:], rows(base, 0))
         for h in range(1, H):
             nc.sync.dma_start(q_head[h][:], rows(q, h))
             nc.sync.dma_start(k_head[h][:], rows(k, h))
-            nc.sync.dma_start(window[h][:], rows(base, h))
+            nc.sync.dma_start(window[h - 1][:], rows(base, h - 1))
+        nc.sync.dma_start(window[H - 1][:], rows(base, H - 1))
 
         ones_column = held.tile([P, 1], BF16, name="ones_column")
         nc.vector.memset(ones_column[:], 1.0)
         identity = held.tile([P, P], F32, name="identity")
         make_identity(nc, identity[:])
 
-        for h in range(H):
-            wa_h = wa_rows[:, h * D : h * D + 1]
-            wd_h = wd_rows[:, h * D : h * D + 1]
+        s_psum, modulation, e, u_psum, u, r = {}, {}, {}, {}, {}, {}
 
-            u_psum = psum_u.tile([P, N], F32, name="u_psum")
-            e_block = []
-            for b in range(KEY_BLOCKS):
-                s_psum = psum_s.tile([P, N], F32, name="s_psum")
-                nc.tensor.matmul(s_psum[:], lhsT=k_head[h][:, b * P : (b + 1) * P], rhs=q_head[h][:], start=True, stop=True)
+        def begin(i):
+            h, b = divmod(i, KEY_BLOCKS)
+            s_psum[i] = psum_s.tile([P, N], F32, name="s_psum")
+            nc.tensor.matmul(s_psum[i][:], lhsT=k_head[h][:, b * P : (b + 1) * P], rhs=q_head[h][:], start=True, stop=True)
+            adj_part = work.tile([P, N], F32, name="adj_part")
+            nc.scalar.activation(adj_part[:], adj_block[b][:], ACT.Identity, bias=1.0, scale=wa_heads[:, h : h + 1])
+            modulation[i] = work.tile([P, N], F32, name="modulation")
+            nc.vector.scalar_tensor_tensor(modulation[i][:], dist_block[b][:], wd_heads[:, h : h + 1], adj_part[:], MULT, ADD)
 
-                adj_part = work.tile([P, N], F32, name="adj_part")
-                nc.scalar.activation(adj_part[:], adj_block[b][:], ACT.Identity, bias=1.0, scale=wa_h)
-                modulation = work.tile([P, N], F32, name="modulation")
-                nc.vector.scalar_tensor_tensor(modulation[:], dist_block[b][:], wd_h, adj_part[:], MULT, ADD)
-                modulated = work.tile([P, N], F32, name="modulated")
-                nc.vector.tensor_tensor(modulated[:], s_psum[:], modulation[:], MULT)
+        def exponentiate(i):
+            modulated = work.tile([P, N], F32, name="modulated")
+            nc.vector.tensor_tensor(modulated[:], s_psum[i][:], modulation[i][:], MULT)
+            e[i] = exps.tile([P, N], BF16, name="e")
+            nc.scalar.activation(e[i][:], modulated[:], ACT.Exp, scale=1.0 / math.sqrt(D))
 
-                e = exps.tile([P, N], BF16, name="e")
-                nc.scalar.activation(e[:], modulated[:], ACT.Exp, scale=1.0 / math.sqrt(D))
-                e_block.append(e)
-                nc.tensor.matmul(u_psum[:], lhsT=v_block[b][:, h * D : (h + 1) * D], rhs=e[:], start=(b == 0), stop=(b == KEY_BLOCKS - 1))
+        def accumulate(i):
+            h, b = divmod(i, KEY_BLOCKS)
+            if b == 0:
+                u_psum[h] = psum_u.tile([P, N], F32, name="u_psum")
+            nc.tensor.matmul(u_psum[h][:], lhsT=v_block[b][:, h * D : (h + 1) * D], rhs=e[i][:], start=(b == 0), stop=(b == KEY_BLOCKS - 1))
 
+        def normalise(h):
             sums_psum = psum_z.tile([P, QUERY_BLOCKS], F32, name="sums_psum")
             for c in range(QUERY_BLOCKS):
                 for b in range(KEY_BLOCKS):
-                    nc.tensor.matmul(sums_psum[:, c : c + 1], lhsT=e_block[b][:, c * P : (c + 1) * P], rhs=ones_column[:], start=(b == 0), stop=(b == KEY_BLOCKS - 1))
+                    nc.tensor.matmul(sums_psum[:, c : c + 1], lhsT=e[h * KEY_BLOCKS + b][:, c * P : (c + 1) * P], rhs=ones_column[:], start=(b == 0), stop=(b == KEY_BLOCKS - 1))
             r_columns = tails.tile([P, QUERY_BLOCKS], F32, name="r_columns")
             nc.vector.reciprocal(r_columns[:], sums_psum[:])
             r_psum = psum_r.tile([P, N], F32, name="r_psum")
             for c in range(QUERY_BLOCKS):
                 nc.tensor.transpose(r_psum[:, c * P : (c + 1) * P], r_columns[:, c : c + 1].to_broadcast([P, P]), identity[:])
+            u[h] = tails.tile([P, N], F32, name="u")
+            nc.scalar.copy(u[h][:], u_psum[h][:])
+            r[h] = tails.tile([P, N], F32, name="r")
+            nc.scalar.copy(r[h][:], r_psum[:])
 
-            u = tails.tile([P, N], F32, name="u")
-            nc.scalar.copy(u[:], u_psum[:])
-            r = tails.tile([P, N], F32, name="r")
-            nc.scalar.copy(r[:], r_psum[:])
-            nc.vector.tensor_tensor(window[h][:].indirect(offsets[:]), u[:], r[:], MULT)
+        def place(h):
+            nc.vector.tensor_tensor(window[h][:].indirect(offsets[:]), u[h][:], r[h][:], MULT)
             nc.sync.dma_start(rows(out, h), window[h][:])
+
+        for step in range(BLOCKS + 2):
+            if step < BLOCKS:
+                begin(step)
+            if 1 <= step <= BLOCKS:
+                exponentiate(step - 1)
+            if step >= 2:
+                accumulate(step - 2)
+                h, b = divmod(step - 2, KEY_BLOCKS)
+                if b == KEY_BLOCKS - 1:
+                    normalise(h)
+                    if h > 0:
+                        place(h - 1)
+        place(H - 1)

@@ -24,6 +24,7 @@ def tile_msrsa_kernel(tc, base, q, k, v, adj, dist, wa, wd, offs, out):
     with (
         tc.tile_pool(name="held", bufs=1) as held,
         tc.tile_pool(name="work", bufs=3) as work,
+        tc.tile_pool(name="mods", bufs=6) as mods,
         tc.tile_pool(name="exps", bufs=2 * KEY_BLOCKS) as exps,
         tc.tile_pool(name="tails", bufs=2) as tails,
         tc.psum_pool(name="psum_s", bufs=3) as psum_s,
@@ -66,14 +67,22 @@ def tile_msrsa_kernel(tc, base, q, k, v, adj, dist, wa, wd, offs, out):
 
         s_psum, modulation, e, u_psum, u, r = {}, {}, {}, {}, {}, {}
 
-        def begin(i):
+        def modulate(i):
+            h, b = divmod(i, KEY_BLOCKS)
+            adj_part = work.tile([P, N], F32, name="adj_part")
+            nc.scalar.activation(adj_part[:], adj_block[b][:], ACT.Identity, bias=1.0, scale=wa_heads[:, h : h + 1])
+            modulation[i] = mods.tile([P, N], F32, name="modulation")
+            if b % 2 == 0:
+                nc.vector.scalar_tensor_tensor(modulation[i][:], dist_block[b][:], wd_heads[:, h : h + 1], adj_part[:], MULT, ADD)
+            else:
+                dist_part = work.tile([P, N], F32, name="dist_part")
+                nc.gpsimd.tensor_scalar(dist_part[:], dist_block[b][:], wd_heads[:, h : h + 1], 0.0, MULT, ADD)
+                nc.gpsimd.tensor_tensor(modulation[i][:], adj_part[:], dist_part[:], ADD)
+
+        def scores(i):
             h, b = divmod(i, KEY_BLOCKS)
             s_psum[i] = psum_s.tile([P, N], F32, name="s_psum")
             nc.tensor.matmul(s_psum[i][:], lhsT=k_head[h][:, b * P : (b + 1) * P], rhs=q_head[h][:], start=True, stop=True)
-            adj_part = work.tile([P, N], F32, name="adj_part")
-            nc.scalar.activation(adj_part[:], adj_block[b][:], ACT.Identity, bias=1.0, scale=wa_heads[:, h : h + 1])
-            modulation[i] = work.tile([P, N], F32, name="modulation")
-            nc.vector.scalar_tensor_tensor(modulation[i][:], dist_block[b][:], wd_heads[:, h : h + 1], adj_part[:], MULT, ADD)
 
         def exponentiate(i):
             modulated = work.tile([P, N], F32, name="modulated")
@@ -106,14 +115,16 @@ def tile_msrsa_kernel(tc, base, q, k, v, adj, dist, wa, wd, offs, out):
             nc.vector.tensor_tensor(window[h][:].indirect(offsets[:]), u[h][:], r[h][:], MULT)
             nc.sync.dma_start(rows(out, h), window[h][:])
 
-        for step in range(BLOCKS + 2):
+        for step in range(BLOCKS + 4):
             if step < BLOCKS:
-                begin(step)
-            if 1 <= step <= BLOCKS:
-                exponentiate(step - 1)
-            if step >= 2:
-                accumulate(step - 2)
-                h, b = divmod(step - 2, KEY_BLOCKS)
+                modulate(step)
+            if 0 <= step - 2 < BLOCKS:
+                scores(step - 2)
+            if 0 <= step - 3 < BLOCKS:
+                exponentiate(step - 3)
+            if step >= 4:
+                accumulate(step - 4)
+                h, b = divmod(step - 4, KEY_BLOCKS)
                 if b == KEY_BLOCKS - 1:
                     normalise(h)
                     if h > 0:

@@ -7,7 +7,6 @@ H, D, T, S, N = 4, 128, 512, 2048, 512
 P = 128
 KEY_BLOCKS = T // P
 QUERY_BLOCKS = N // P
-BLOCKS = H * KEY_BLOCKS
 FLOPS = 4 * H * D * T * N
 
 F32, BF16, U16 = mybir.dt.float32, mybir.dt.bfloat16, mybir.dt.uint16
@@ -23,23 +22,17 @@ def tile_msrsa_kernel(tc, base, q, k, v, adj, dist, wa, wd, offs, out):
     nc = tc.nc
     with (
         tc.tile_pool(name="held", bufs=1) as held,
-        tc.tile_pool(name="work", bufs=3) as work,
-        tc.tile_pool(name="mods", bufs=6) as mods,
-        tc.tile_pool(name="exps", bufs=2 * KEY_BLOCKS) as exps,
-        tc.tile_pool(name="tails", bufs=2) as tails,
-        tc.psum_pool(name="psum_s", bufs=3) as psum_s,
+        tc.tile_pool(name="work", bufs=4) as work,
+        tc.psum_pool(name="psum_small", bufs=1) as psum_small,
+        tc.psum_pool(name="psum_s", bufs=KEY_BLOCKS) as psum_s,
         tc.psum_pool(name="psum_u", bufs=2) as psum_u,
-        tc.psum_pool(name="psum_z", bufs=1) as psum_z,
-        tc.psum_pool(name="psum_r", bufs=2) as psum_r,
+        tc.psum_pool(name="psum_r", bufs=1) as psum_r,
     ):
-        offsets = held.tile([P, N // 16], U16, name="offsets")
-        nc.sync.dma_start(offsets[:], offs)
-
-        wa_heads = held.tile([P, H], F32, name="wa_heads")
-        wd_heads = held.tile([P, H], F32, name="wd_heads")
-        with nc.allow_non_contiguous_dma(reason="two loads of 512 single float32 values"):
-            nc.scalar.dma_start(wa_heads[:], wa.rearrange("(h d) o -> d (h o)", d=D))
-            nc.scalar.dma_start(wd_heads[:], wd.rearrange("(h d) o -> d (h o)", d=D))
+        wa_row = held.tile([1, H], F32, name="wa_row")
+        wd_row = held.tile([1, H], F32, name="wd_row")
+        with nc.allow_non_contiguous_dma(reason="four single float32 values each"):
+            nc.sync.dma_start(wa_row[:], wa.rearrange("(h d) o -> d (h o)", d=D)[0:1, :])
+            nc.scalar.dma_start(wd_row[:], wd.rearrange("(h d) o -> d (h o)", d=D)[0:1, :])
 
         q_head = [held.tile([P, N], BF16, name=f"q_head{h}") for h in range(H)]
         k_head = [held.tile([P, T], BF16, name=f"k_head{h}") for h in range(H)]
@@ -47,86 +40,103 @@ def tile_msrsa_kernel(tc, base, q, k, v, adj, dist, wa, wd, offs, out):
         adj_block = [held.tile([P, N], F32, name=f"adj_block{b}") for b in range(KEY_BLOCKS)]
         dist_block = [held.tile([P, N], F32, name=f"dist_block{b}") for b in range(KEY_BLOCKS)]
         v_block = [held.tile([P, H * D], BF16, name=f"v_block{b}") for b in range(KEY_BLOCKS)]
+        offsets = held.tile([P, N // 16], U16, name="offsets")
 
-        nc.sync.dma_start(q_head[0][:], rows(q, 0))
-        nc.sync.dma_start(k_head[0][:], rows(k, 0))
         for b in range(KEY_BLOCKS):
             nc.sync.dma_start(adj_block[b][:], rows(adj, b))
             nc.sync.dma_start(dist_block[b][:], rows(dist, b))
+        nc.sync.dma_start(q_head[0][:], rows(q, 0))
+        nc.sync.dma_start(k_head[0][:], rows(k, 0))
+        for b in range(KEY_BLOCKS):
             nc.sync.dma_start(v_block[b][:], rows(v, b))
         for h in range(1, H):
             nc.sync.dma_start(q_head[h][:], rows(q, h))
             nc.sync.dma_start(k_head[h][:], rows(k, h))
-            nc.sync.dma_start(window[h - 1][:], rows(base, h - 1))
-        nc.sync.dma_start(window[H - 1][:], rows(base, H - 1))
+        nc.sync.dma_start(offsets[:], offs)
+        for h in range(H):
+            nc.sync.dma_start(window[h][:], rows(base, h))
 
         ones_column = held.tile([P, 1], BF16, name="ones_column")
-        nc.vector.memset(ones_column[:], 1.0)
+        nc.gpsimd.memset(ones_column[:], 1.0)
+        ones_row = held.tile([1, P], F32, name="ones_row")
+        nc.gpsimd.memset(ones_row[:], 1.0)
         identity = held.tile([P, P], F32, name="identity")
         make_identity(nc, identity[:])
 
-        s_psum, modulation, e, u_psum, u, r = {}, {}, {}, {}, {}, {}
+        weights_psum = psum_small.tile([P, 2 * H], F32, name="weights_psum", tag="small")
+        nc.tensor.matmul(weights_psum[:, 0:H], lhsT=ones_row[:], rhs=wa_row[:], start=True, stop=True)
+        nc.tensor.matmul(weights_psum[:, H : 2 * H], lhsT=ones_row[:], rhs=wd_row[:], start=True, stop=True)
+        weights = held.tile([P, 2 * H], F32, name="weights")
+        nc.vector.tensor_copy(weights[:], weights_psum[:])
+        wa_heads, wd_heads = weights[:, 0:H], weights[:, H : 2 * H]
 
-        def modulate(i):
-            h, b = divmod(i, KEY_BLOCKS)
-            adj_part = work.tile([P, N], F32, name="adj_part")
-            nc.scalar.activation(adj_part[:], adj_block[b][:], ACT.Identity, bias=1.0, scale=wa_heads[:, h : h + 1])
-            modulation[i] = mods.tile([P, N], F32, name="modulation")
-            if b % 2 == 0:
-                nc.vector.scalar_tensor_tensor(modulation[i][:], dist_block[b][:], wd_heads[:, h : h + 1], adj_part[:], MULT, ADD)
-            else:
-                dist_part = work.tile([P, N], F32, name="dist_part")
-                nc.gpsimd.tensor_scalar(dist_part[:], dist_block[b][:], wd_heads[:, h : h + 1], 0.0, MULT, ADD)
-                nc.gpsimd.tensor_tensor(modulation[i][:], adj_part[:], dist_part[:], ADD)
+        modulation = {(h, b): held.tile([P, N], F32, name=f"modulation{h}_{b}") for h in range(H) for b in range(KEY_BLOCKS)}
+        u = [held.tile([P, N], F32, name=f"u{h}") for h in range(H)]
+        r = [held.tile([P, N], F32, name=f"r{h}") for h in range(H)]
+        modulated = {(h, b): held.tile([P, N], F32, name=f"modulated{h}_{b}") for h in range(H) for b in range(KEY_BLOCKS)}
+        e = {(h, b): held.tile([P, N], BF16, name=f"e{h}_{b}") for h in range(H) for b in range(KEY_BLOCKS)}
+        adj_part, s_psum, u_psum, sums_psum = {}, {}, {}, {}
 
-        def scores(i):
-            h, b = divmod(i, KEY_BLOCKS)
-            s_psum[i] = psum_s.tile([P, N], F32, name="s_psum")
-            nc.tensor.matmul(s_psum[i][:], lhsT=k_head[h][:, b * P : (b + 1) * P], rhs=q_head[h][:], start=True, stop=True)
+        def start_modulation(h, b):
+            adj_part[h, b] = work.tile([P, N], F32, name="adj_part")
+            nc.scalar.activation(adj_part[h, b][:], adj_block[b][:], ACT.Identity, bias=1.0, scale=wa_heads[:, h : h + 1])
 
-        def exponentiate(i):
-            modulated = work.tile([P, N], F32, name="modulated")
-            nc.vector.tensor_tensor(modulated[:], s_psum[i][:], modulation[i][:], MULT)
-            e[i] = exps.tile([P, N], BF16, name="e")
-            nc.scalar.activation(e[i][:], modulated[:], ACT.Exp, scale=1.0 / math.sqrt(D))
+        def finish_modulation(h, b):
+            nc.vector.scalar_tensor_tensor(modulation[h, b][:], dist_block[b][:], wd_heads[:, h : h + 1], adj_part[h, b][:], MULT, ADD)
 
-        def accumulate(i):
-            h, b = divmod(i, KEY_BLOCKS)
+        def scores(h, b):
+            s_psum[h, b] = psum_s.tile([P, N], F32, name="s_psum")
+            nc.tensor.matmul(s_psum[h, b][:], lhsT=k_head[h][:, b * P : (b + 1) * P], rhs=q_head[h][:], start=True, stop=True)
+
+        def exponentiate(h, b):
+            nc.vector.tensor_tensor(modulated[h, b][:], s_psum[h, b][:], modulation[h, b][:], MULT)
+            nc.scalar.activation(e[h, b][:], modulated[h, b][:], ACT.Exp, scale=1.0 / math.sqrt(D))
+
+        def accumulate(h, b):
             if b == 0:
                 u_psum[h] = psum_u.tile([P, N], F32, name="u_psum")
-            nc.tensor.matmul(u_psum[h][:], lhsT=v_block[b][:, h * D : (h + 1) * D], rhs=e[i][:], start=(b == 0), stop=(b == KEY_BLOCKS - 1))
+            nc.tensor.matmul(u_psum[h][:], lhsT=v_block[b][:, h * D : (h + 1) * D], rhs=e[h, b][:], start=(b == 0), stop=(b == KEY_BLOCKS - 1))
 
-        def normalise(h):
-            sums_psum = psum_z.tile([P, QUERY_BLOCKS], F32, name="sums_psum")
+        def finish_sums(h):
+            sums_psum[h] = psum_small.tile([P, QUERY_BLOCKS], F32, name="sums_psum", tag="small")
             for c in range(QUERY_BLOCKS):
                 for b in range(KEY_BLOCKS):
-                    nc.tensor.matmul(sums_psum[:, c : c + 1], lhsT=e[h * KEY_BLOCKS + b][:, c * P : (c + 1) * P], rhs=ones_column[:], start=(b == 0), stop=(b == KEY_BLOCKS - 1))
-            r_columns = tails.tile([P, QUERY_BLOCKS], F32, name="r_columns")
-            nc.vector.reciprocal(r_columns[:], sums_psum[:])
+                    nc.tensor.matmul(sums_psum[h][:, c : c + 1], lhsT=e[h, b][:, c * P : (c + 1) * P], rhs=ones_column[:], start=(b == 0), stop=(b == KEY_BLOCKS - 1))
+
+        def invert_sums(h):
+            r_columns = work.tile([P, QUERY_BLOCKS], F32, name="r_columns")
+            nc.vector.reciprocal(r_columns[:], sums_psum[h][:])
             r_psum = psum_r.tile([P, N], F32, name="r_psum")
             for c in range(QUERY_BLOCKS):
                 nc.tensor.transpose(r_psum[:, c * P : (c + 1) * P], r_columns[:, c : c + 1].to_broadcast([P, P]), identity[:])
-            u[h] = tails.tile([P, N], F32, name="u")
-            nc.scalar.copy(u[h][:], u_psum[h][:])
-            r[h] = tails.tile([P, N], F32, name="r")
             nc.scalar.copy(r[h][:], r_psum[:])
+            nc.scalar.copy(u[h][:], u_psum[h][:])
 
         def place(h):
             nc.vector.tensor_tensor(window[h][:].indirect(offsets[:]), u[h][:], r[h][:], MULT)
             nc.sync.dma_start(rows(out, h), window[h][:])
 
-        for step in range(BLOCKS + 4):
-            if step < BLOCKS:
-                modulate(step)
-            if 0 <= step - 2 < BLOCKS:
-                scores(step - 2)
-            if 0 <= step - 3 < BLOCKS:
-                exponentiate(step - 3)
-            if step >= 4:
-                accumulate(step - 4)
-                h, b = divmod(step - 4, KEY_BLOCKS)
-                if b == KEY_BLOCKS - 1:
-                    normalise(h)
-                    if h > 0:
-                        place(h - 1)
+        for b in range(KEY_BLOCKS):
+            for h in range(2):
+                start_modulation(h, b)
+                finish_modulation(h, b)
+        for b in range(KEY_BLOCKS):
+            scores(0, b)
+        for h in range(H):
+            for b in range(KEY_BLOCKS):
+                if h + 2 < H:
+                    start_modulation(h + 2, b)
+                exponentiate(h, b)
+                if h + 1 < H:
+                    scores(h + 1, b)
+                accumulate(h, b)
+                if h + 2 < H:
+                    finish_modulation(h + 2, b)
+            if h >= 1:
+                invert_sums(h - 1)
+            finish_sums(h)
+            if h >= 2:
+                place(h - 2)
+        invert_sums(H - 1)
+        place(H - 2)
         place(H - 1)

@@ -23,8 +23,8 @@ def tile_msrsa_kernel(tc, base, q, k, v, adj, dist, wa, wd, offs, out):
     with (
         tc.tile_pool(name="held", bufs=1) as held,
         tc.tile_pool(name="work", bufs=4) as work,
-        tc.psum_pool(name="psum_small", bufs=1) as psum_small,
         tc.psum_pool(name="psum_s", bufs=KEY_BLOCKS) as psum_s,
+        tc.psum_pool(name="psum_sums", bufs=1) as psum_sums,
         tc.psum_pool(name="psum_u", bufs=2) as psum_u,
         tc.psum_pool(name="psum_r", bufs=1) as psum_r,
     ):
@@ -56,26 +56,29 @@ def tile_msrsa_kernel(tc, base, q, k, v, adj, dist, wa, wd, offs, out):
         for h in range(H):
             nc.sync.dma_start(window[h][:], rows(base, h))
 
-        ones_column = held.tile([P, 1], BF16, name="ones_column")
-        nc.gpsimd.memset(ones_column[:], 1.0)
         ones_row = held.tile([1, P], F32, name="ones_row")
         nc.gpsimd.memset(ones_row[:], 1.0)
+        zero_column = held.tile([P, 1], F32, name="zero_column")
+        nc.gpsimd.memset(zero_column[:], 0.0)
         identity = held.tile([P, P], F32, name="identity")
         make_identity(nc, identity[:])
+        ones_column = held.tile([P, 1], BF16, name="ones_column")
+        nc.scalar.activation(ones_column[:], zero_column[:], ACT.Exp)
 
-        weights_psum = psum_small.tile([P, 2 * H], F32, name="weights_psum", tag="small")
-        nc.tensor.matmul(weights_psum[:, 0:H], lhsT=ones_row[:], rhs=wa_row[:], start=True, stop=True)
-        nc.tensor.matmul(weights_psum[:, H : 2 * H], lhsT=ones_row[:], rhs=wd_row[:], start=True, stop=True)
-        weights = held.tile([P, 2 * H], F32, name="weights")
-        nc.vector.tensor_copy(weights[:], weights_psum[:])
-        wa_heads, wd_heads = weights[:, 0:H], weights[:, H : 2 * H]
+        wa_heads = held.tile([P, H], F32, name="wa_heads")
+        wd_heads = held.tile([P, H], F32, name="wd_heads")
+        for row, heads in ((wa_row, wa_heads), (wd_row, wd_heads)):
+            heads_psum = psum_r.tile([P, H], F32, name="heads_psum", tag="r_psum")
+            nc.tensor.matmul(heads_psum[:], lhsT=ones_row[:], rhs=row[:], start=True, stop=True)
+            nc.vector.tensor_copy(heads[:], heads_psum[:])
 
         modulation = {(h, b): held.tile([P, N], F32, name=f"modulation{h}_{b}") for h in range(H) for b in range(KEY_BLOCKS)}
         u = [held.tile([P, N], F32, name=f"u{h}") for h in range(H)]
         r = [held.tile([P, N], F32, name=f"r{h}") for h in range(H)]
         modulated = {(h, b): held.tile([P, N], F32, name=f"modulated{h}_{b}") for h in range(H) for b in range(KEY_BLOCKS)}
         e = {(h, b): held.tile([P, N], BF16, name=f"e{h}_{b}") for h in range(H) for b in range(KEY_BLOCKS)}
-        adj_part, s_psum, u_psum, sums_psum = {}, {}, {}, {}
+        sums_psum = psum_sums.tile([P, H, QUERY_BLOCKS, KEY_BLOCKS], F32, name="sums_psum")
+        adj_part, s_psum, u_psum = {}, {}, {}
 
         def start_modulation(h, b):
             adj_part[h, b] = work.tile([P, N], F32, name="adj_part")
@@ -95,18 +98,16 @@ def tile_msrsa_kernel(tc, base, q, k, v, adj, dist, wa, wd, offs, out):
         def accumulate(h, b):
             if b == 0:
                 u_psum[h] = psum_u.tile([P, N], F32, name="u_psum")
+            for c in range(QUERY_BLOCKS):
+                nc.tensor.matmul(sums_psum[:, h, c, b : b + 1], lhsT=e[h, b][:, c * P : (c + 1) * P], rhs=ones_column[:], start=True, stop=True)
             nc.tensor.matmul(u_psum[h][:], lhsT=v_block[b][:, h * D : (h + 1) * D], rhs=e[h, b][:], start=(b == 0), stop=(b == KEY_BLOCKS - 1))
 
-        def finish_sums(h):
-            sums_psum[h] = psum_small.tile([P, QUERY_BLOCKS], F32, name="sums_psum", tag="small")
-            for c in range(QUERY_BLOCKS):
-                for b in range(KEY_BLOCKS):
-                    nc.tensor.matmul(sums_psum[h][:, c : c + 1], lhsT=e[h, b][:, c * P : (c + 1) * P], rhs=ones_column[:], start=(b == 0), stop=(b == KEY_BLOCKS - 1))
-
         def invert_sums(h):
+            sums = work.tile([P, QUERY_BLOCKS], F32, name="sums")
+            nc.vector.reduce_sum(sums[:], sums_psum[:, h, :, :], axis=mybir.AxisListType.X)
             r_columns = work.tile([P, QUERY_BLOCKS], F32, name="r_columns")
-            nc.vector.reciprocal(r_columns[:], sums_psum[h][:])
-            r_psum = psum_r.tile([P, N], F32, name="r_psum")
+            nc.vector.reciprocal(r_columns[:], sums[:])
+            r_psum = psum_r.tile([P, N], F32, name="r_psum", tag="r_psum")
             for c in range(QUERY_BLOCKS):
                 nc.tensor.transpose(r_psum[:, c * P : (c + 1) * P], r_columns[:, c : c + 1].to_broadcast([P, P]), identity[:])
             nc.scalar.copy(r[h][:], r_psum[:])
@@ -134,7 +135,6 @@ def tile_msrsa_kernel(tc, base, q, k, v, adj, dist, wa, wd, offs, out):
                     finish_modulation(h + 2, b)
             if h >= 1:
                 invert_sums(h - 1)
-            finish_sums(h)
             if h >= 2:
                 place(h - 2)
         invert_sums(H - 1)

@@ -7,6 +7,8 @@ H, D, T, S, N = 4, 128, 512, 2048, 512
 P = 128
 KEY_BLOCKS = T // P
 QUERY_BLOCKS = N // P
+MODULATION_AHEAD = 2
+PLACING_LATE = 2
 FLOPS = 4 * H * D * T * N
 
 F32, BF16, U16 = mybir.dt.float32, mybir.dt.bfloat16, mybir.dt.uint16
@@ -24,8 +26,8 @@ def tile_msrsa_kernel(tc, base, q, k, v, adj, dist, wa, wd, offs, out):
         tc.tile_pool(name="held", bufs=1) as held,
         tc.tile_pool(name="work", bufs=4) as work,
         tc.psum_pool(name="psum_s", bufs=KEY_BLOCKS) as psum_s,
-        tc.psum_pool(name="psum_sums", bufs=1) as psum_sums,
         tc.psum_pool(name="psum_u", bufs=2) as psum_u,
+        tc.psum_pool(name="psum_small", bufs=1) as psum_small,
         tc.psum_pool(name="psum_r", bufs=1) as psum_r,
     ):
         wa_row = held.tile([1, H], F32, name="wa_row")
@@ -68,17 +70,17 @@ def tile_msrsa_kernel(tc, base, q, k, v, adj, dist, wa, wd, offs, out):
         wa_heads = held.tile([P, H], F32, name="wa_heads")
         wd_heads = held.tile([P, H], F32, name="wd_heads")
         for row, heads in ((wa_row, wa_heads), (wd_row, wd_heads)):
-            heads_psum = psum_r.tile([P, H], F32, name="heads_psum", tag="r_psum")
+            heads_psum = psum_small.tile([P, H], F32, name="heads_psum", tag="small")
             nc.tensor.matmul(heads_psum[:], lhsT=ones_row[:], rhs=row[:], start=True, stop=True)
             nc.vector.tensor_copy(heads[:], heads_psum[:])
 
-        modulation = {(h, b): held.tile([P, N], F32, name=f"modulation{h}_{b}") for h in range(H) for b in range(KEY_BLOCKS)}
+        blocks = [(h, b) for h in range(H) for b in range(KEY_BLOCKS)]
+        modulation = {hb: held.tile([P, N], F32, name=f"modulation{hb[0]}_{hb[1]}") for hb in blocks}
+        modulated = {hb: held.tile([P, N], F32, name=f"modulated{hb[0]}_{hb[1]}") for hb in blocks}
+        e = {hb: held.tile([P, N], BF16, name=f"e{hb[0]}_{hb[1]}") for hb in blocks}
         u = [held.tile([P, N], F32, name=f"u{h}") for h in range(H)]
         r = [held.tile([P, N], F32, name=f"r{h}") for h in range(H)]
-        modulated = {(h, b): held.tile([P, N], F32, name=f"modulated{h}_{b}") for h in range(H) for b in range(KEY_BLOCKS)}
-        e = {(h, b): held.tile([P, N], BF16, name=f"e{h}_{b}") for h in range(H) for b in range(KEY_BLOCKS)}
-        sums_psum = psum_sums.tile([P, H, QUERY_BLOCKS, KEY_BLOCKS], F32, name="sums_psum")
-        adj_part, s_psum, u_psum = {}, {}, {}
+        adj_part, s_psum, u_psum, sums_psum = {}, {}, {}, {}
 
         def start_modulation(h, b):
             adj_part[h, b] = work.tile([P, N], F32, name="adj_part")
@@ -98,16 +100,18 @@ def tile_msrsa_kernel(tc, base, q, k, v, adj, dist, wa, wd, offs, out):
         def accumulate(h, b):
             if b == 0:
                 u_psum[h] = psum_u.tile([P, N], F32, name="u_psum")
-            for c in range(QUERY_BLOCKS):
-                nc.tensor.matmul(sums_psum[:, h, c, b : b + 1], lhsT=e[h, b][:, c * P : (c + 1) * P], rhs=ones_column[:], start=True, stop=True)
             nc.tensor.matmul(u_psum[h][:], lhsT=v_block[b][:, h * D : (h + 1) * D], rhs=e[h, b][:], start=(b == 0), stop=(b == KEY_BLOCKS - 1))
 
+        def sum_exponentials(h):
+            sums_psum[h] = psum_small.tile([P, QUERY_BLOCKS], F32, name="sums_psum", tag="small")
+            for c in range(QUERY_BLOCKS):
+                for b in range(KEY_BLOCKS):
+                    nc.tensor.matmul(sums_psum[h][:, c : c + 1], lhsT=e[h, b][:, c * P : (c + 1) * P], rhs=ones_column[:], start=(b == 0), stop=(b == KEY_BLOCKS - 1))
+
         def invert_sums(h):
-            sums = work.tile([P, QUERY_BLOCKS], F32, name="sums")
-            nc.vector.reduce_sum(sums[:], sums_psum[:, h, :, :], axis=mybir.AxisListType.X)
             r_columns = work.tile([P, QUERY_BLOCKS], F32, name="r_columns")
-            nc.vector.reciprocal(r_columns[:], sums[:])
-            r_psum = psum_r.tile([P, N], F32, name="r_psum", tag="r_psum")
+            nc.vector.reciprocal(r_columns[:], sums_psum[h][:])
+            r_psum = psum_r.tile([P, N], F32, name="r_psum")
             for c in range(QUERY_BLOCKS):
                 nc.tensor.transpose(r_psum[:, c * P : (c + 1) * P], r_columns[:, c : c + 1].to_broadcast([P, P]), identity[:])
             nc.scalar.copy(r[h][:], r_psum[:])
@@ -118,25 +122,26 @@ def tile_msrsa_kernel(tc, base, q, k, v, adj, dist, wa, wd, offs, out):
             nc.sync.dma_start(rows(out, h), window[h][:])
 
         for b in range(KEY_BLOCKS):
-            for h in range(2):
+            for h in range(MODULATION_AHEAD):
                 start_modulation(h, b)
                 finish_modulation(h, b)
         for b in range(KEY_BLOCKS):
             scores(0, b)
         for h in range(H):
             for b in range(KEY_BLOCKS):
-                if h + 2 < H:
-                    start_modulation(h + 2, b)
+                if h + MODULATION_AHEAD < H:
+                    start_modulation(h + MODULATION_AHEAD, b)
                 exponentiate(h, b)
                 if h + 1 < H:
                     scores(h + 1, b)
                 accumulate(h, b)
-                if h + 2 < H:
-                    finish_modulation(h + 2, b)
+                if h + MODULATION_AHEAD < H:
+                    finish_modulation(h + MODULATION_AHEAD, b)
             if h >= 1:
                 invert_sums(h - 1)
-            if h >= 2:
-                place(h - 2)
+            sum_exponentials(h)
+            if h >= PLACING_LATE:
+                place(h - PLACING_LATE)
         invert_sums(H - 1)
-        place(H - 2)
-        place(H - 1)
+        for h in range(H - PLACING_LATE, H):
+            place(h)

@@ -7,12 +7,12 @@ H, D, T, S, N = 4, 128, 512, 2048, 512
 P = 128
 KEY_BLOCKS = T // P
 QUERY_BLOCKS = N // P
-MODULATION_AHEAD = 2
-PLACING_LATE = 2
+MODULATION_AHEAD = 1
 FLOPS = 4 * H * D * T * N
+HUGE = 1e18
 
 F32, BF16, U16 = mybir.dt.float32, mybir.dt.bfloat16, mybir.dt.uint16
-MULT, ADD = mybir.AluOpType.mult, mybir.AluOpType.add
+MULT, ADD, MIN, MAX = mybir.AluOpType.mult, mybir.AluOpType.add, mybir.AluOpType.min, mybir.AluOpType.max
 ACT = mybir.ActivationFunctionType
 
 
@@ -47,8 +47,9 @@ def tile_msrsa_kernel(tc, base, q, k, v, adj, dist, wa, wd, offs, out):
         for b in range(KEY_BLOCKS):
             nc.sync.dma_start(adj_block[b][:], rows(adj, b))
             nc.sync.dma_start(dist_block[b][:], rows(dist, b))
-        nc.sync.dma_start(q_head[0][:], rows(q, 0))
-        nc.sync.dma_start(k_head[0][:], rows(k, 0))
+            if b == 0:
+                nc.sync.dma_start(q_head[0][:], rows(q, 0))
+                nc.sync.dma_start(k_head[0][:], rows(k, 0))
         for b in range(KEY_BLOCKS):
             nc.sync.dma_start(v_block[b][:], rows(v, b))
         for h in range(1, H):
@@ -67,12 +68,30 @@ def tile_msrsa_kernel(tc, base, q, k, v, adj, dist, wa, wd, offs, out):
         ones_column = held.tile([P, 1], BF16, name="ones_column")
         nc.scalar.activation(ones_column[:], zero_column[:], ACT.Exp)
 
-        wa_heads = held.tile([P, H], F32, name="wa_heads")
-        wd_heads = held.tile([P, H], F32, name="wd_heads")
-        for row, heads in ((wa_row, wa_heads), (wd_row, wd_heads)):
-            heads_psum = psum_small.tile([P, H], F32, name="heads_psum", tag="small")
-            nc.tensor.matmul(heads_psum[:], lhsT=ones_row[:], rhs=row[:], start=True, stop=True)
-            nc.vector.tensor_copy(heads[:], heads_psum[:])
+        inverse = held.tile([1, H], F32, name="inverse")
+        head_row = held.tile([1, 2 * H], F32, name="head_row")
+        nc.vector.reciprocal(inverse[:], wd_row[:])
+        nc.vector.tensor_scalar(head_row[:, H : 2 * H], inverse[:], HUGE, -HUGE, MIN, MAX)
+        nc.vector.tensor_tensor(head_row[:, 0:H], wa_row[:], head_row[:, H : 2 * H], MULT)
+        head_numbers = held.tile([P, 2 * H], F32, name="head_numbers")
+        heads_psum = psum_small.tile([P, 2 * H], F32, name="heads_psum", tag="small")
+        nc.tensor.matmul(heads_psum[:], lhsT=ones_row[:], rhs=head_row[:], start=True, stop=True)
+        nc.vector.tensor_copy(head_numbers[:], heads_psum[:])
+        bounded_wd = held.tile([P, H], F32, name="bounded_wd")
+        exp_scale = held.tile([P, H], F32, name="exp_scale")
+
+        def make_exp_scale():
+            nc.vector.reciprocal(bounded_wd[:], head_numbers[:, H : 2 * H])
+            nc.vector.tensor_scalar_mul(exp_scale[:], bounded_wd[:], 1.0 / math.sqrt(D))
+
+        def wa_over_wd(h):
+            return head_numbers[:, h : h + 1]
+
+        def one_over_wd(h):
+            return head_numbers[:, H + h : H + h + 1]
+
+        def wd_over_root(h):
+            return exp_scale[:, h : h + 1]
 
         blocks = [(h, b) for h in range(H) for b in range(KEY_BLOCKS)]
         modulation = {hb: held.tile([P, N], F32, name=f"modulation{hb[0]}_{hb[1]}") for hb in blocks}
@@ -80,22 +99,18 @@ def tile_msrsa_kernel(tc, base, q, k, v, adj, dist, wa, wd, offs, out):
         e = {hb: held.tile([P, N], BF16, name=f"e{hb[0]}_{hb[1]}") for hb in blocks}
         u = [held.tile([P, N], F32, name=f"u{h}") for h in range(H)]
         r = [held.tile([P, N], F32, name=f"r{h}") for h in range(H)]
-        adj_part, s_psum, u_psum, sums_psum = {}, {}, {}, {}
+        s_psum, u_psum, sums_psum = {}, {}, {}
 
-        def start_modulation(h, b):
-            adj_part[h, b] = work.tile([P, N], F32, name="adj_part")
-            nc.scalar.activation(adj_part[h, b][:], adj_block[b][:], ACT.Identity, bias=1.0, scale=wa_heads[:, h : h + 1])
-
-        def finish_modulation(h, b):
-            nc.vector.scalar_tensor_tensor(modulation[h, b][:], dist_block[b][:], wd_heads[:, h : h + 1], adj_part[h, b][:], MULT, ADD)
+        def modulate(h, b):
+            nc.vector.scalar_tensor_tensor(modulation[h, b][:], adj_block[b][:], wa_over_wd(h), dist_block[b][:], MULT, ADD)
 
         def scores(h, b):
             s_psum[h, b] = psum_s.tile([P, N], F32, name="s_psum")
             nc.tensor.matmul(s_psum[h, b][:], lhsT=k_head[h][:, b * P : (b + 1) * P], rhs=q_head[h][:], start=True, stop=True)
 
         def exponentiate(h, b):
-            nc.vector.tensor_tensor(modulated[h, b][:], s_psum[h, b][:], modulation[h, b][:], MULT)
-            nc.scalar.activation(e[h, b][:], modulated[h, b][:], ACT.Exp, scale=1.0 / math.sqrt(D))
+            nc.vector.scalar_tensor_tensor(modulated[h, b][:], modulation[h, b][:], one_over_wd(h), s_psum[h, b][:], ADD, MULT)
+            nc.scalar.activation(e[h, b][:], modulated[h, b][:], ACT.Exp, scale=wd_over_root(h))
 
         def accumulate(h, b):
             if b == 0:
@@ -123,25 +138,21 @@ def tile_msrsa_kernel(tc, base, q, k, v, adj, dist, wa, wd, offs, out):
 
         for b in range(KEY_BLOCKS):
             for h in range(MODULATION_AHEAD):
-                start_modulation(h, b)
-                finish_modulation(h, b)
+                modulate(h, b)
+        make_exp_scale()
         for b in range(KEY_BLOCKS):
             scores(0, b)
         for h in range(H):
             for b in range(KEY_BLOCKS):
-                if h + MODULATION_AHEAD < H:
-                    start_modulation(h + MODULATION_AHEAD, b)
                 exponentiate(h, b)
                 if h + 1 < H:
                     scores(h + 1, b)
                 accumulate(h, b)
                 if h + MODULATION_AHEAD < H:
-                    finish_modulation(h + MODULATION_AHEAD, b)
+                    modulate(h + MODULATION_AHEAD, b)
             if h >= 1:
                 invert_sums(h - 1)
             sum_exponentials(h)
-            if h >= PLACING_LATE:
-                place(h - PLACING_LATE)
         invert_sums(H - 1)
-        for h in range(H - PLACING_LATE, H):
+        for h in range(H):
             place(h)

@@ -77,12 +77,14 @@ def tile_msrsa_kernel(tc, base, q, k, v, adj, dist, wa, wd, offs, out):
         heads_psum = psum_small.tile([P, 2 * H], F32, name="heads_psum", tag="small")
         nc.tensor.matmul(heads_psum[:], lhsT=ones_row[:], rhs=head_row[:], start=True, stop=True)
         nc.vector.tensor_copy(head_numbers[:], heads_psum[:])
-        bounded_wd = held.tile([P, H], F32, name="bounded_wd")
+        bounded_wd = held.tile([1, H], F32, name="bounded_wd")
+        scale_row = held.tile([1, H], F32, name="scale_row")
+        nc.vector.reciprocal(bounded_wd[:], head_row[:, H : 2 * H])
+        nc.vector.tensor_scalar_mul(scale_row[:], bounded_wd[:], 1.0 / math.sqrt(D))
         exp_scale = held.tile([P, H], F32, name="exp_scale")
-
-        def make_exp_scale():
-            nc.vector.reciprocal(bounded_wd[:], head_numbers[:, H : 2 * H])
-            nc.vector.tensor_scalar_mul(exp_scale[:], bounded_wd[:], 1.0 / math.sqrt(D))
+        scale_psum = psum_r.tile([P, H], F32, name="scale_psum", tag="r_psum")
+        nc.tensor.matmul(scale_psum[:], lhsT=ones_row[:], rhs=scale_row[:], start=True, stop=True)
+        nc.scalar.copy(exp_scale[:], scale_psum[:])
 
         def wa_over_wd(h):
             return head_numbers[:, h : h + 1]
@@ -139,7 +141,6 @@ def tile_msrsa_kernel(tc, base, q, k, v, adj, dist, wa, wd, offs, out):
         for b in range(KEY_BLOCKS):
             for h in range(MODULATION_AHEAD):
                 modulate(h, b)
-        make_exp_scale()
         for b in range(KEY_BLOCKS):
             scores(0, b)
         for h in range(H):

import math

import concourse.mybir as mybir
from concourse.masks import make_identity

H, D, T, S, N = 4, 128, 512, 2048, 512
P = 128
KEY_BLOCKS = T // P
QUERY_BLOCKS = N // P
MODULATION_AHEAD = 1
FLOPS = 4 * H * D * T * N
HUGE = 1e18

F32, BF16, U16 = mybir.dt.float32, mybir.dt.bfloat16, mybir.dt.uint16
MULT, ADD, MIN, MAX = mybir.AluOpType.mult, mybir.AluOpType.add, mybir.AluOpType.min, mybir.AluOpType.max
ACT = mybir.ActivationFunctionType


def rows(dram, i):
    return dram[i * P : (i + 1) * P, :]


def tile_msrsa_kernel(tc, base, q, k, v, adj, dist, wa, wd, offs, out):
    nc = tc.nc
    with (
        tc.tile_pool(name="held", bufs=1) as held,
        tc.tile_pool(name="work", bufs=4) as work,
        tc.psum_pool(name="psum_s", bufs=KEY_BLOCKS) as psum_s,
        tc.psum_pool(name="psum_u", bufs=2) as psum_u,
        tc.psum_pool(name="psum_small", bufs=1) as psum_small,
        tc.psum_pool(name="psum_r", bufs=1) as psum_r,
    ):
        wa_row = held.tile([1, H], F32, name="wa_row")
        wd_row = held.tile([1, H], F32, name="wd_row")
        with nc.allow_non_contiguous_dma(reason="four single float32 values each"):
            nc.sync.dma_start(wa_row[:], wa.rearrange("(h d) o -> d (h o)", d=D)[0:1, :])
            nc.scalar.dma_start(wd_row[:], wd.rearrange("(h d) o -> d (h o)", d=D)[0:1, :])

        q_head = [held.tile([P, N], BF16, name=f"q_head{h}") for h in range(H)]
        k_head = [held.tile([P, T], BF16, name=f"k_head{h}") for h in range(H)]
        window = [held.tile([P, S], F32, name=f"window{h}") for h in range(H)]
        adj_block = [held.tile([P, N], F32, name=f"adj_block{b}") for b in range(KEY_BLOCKS)]
        dist_block = [held.tile([P, N], F32, name=f"dist_block{b}") for b in range(KEY_BLOCKS)]
        v_block = [held.tile([P, H * D], BF16, name=f"v_block{b}") for b in range(KEY_BLOCKS)]
        offsets = held.tile([P, N // 16], U16, name="offsets")

        for b in range(KEY_BLOCKS):
            nc.sync.dma_start(adj_block[b][:], rows(adj, b))
            nc.sync.dma_start(dist_block[b][:], rows(dist, b))
            if b == 0:
                nc.sync.dma_start(q_head[0][:], rows(q, 0))
                nc.sync.dma_start(k_head[0][:], rows(k, 0))
        for b in range(KEY_BLOCKS):
            nc.sync.dma_start(v_block[b][:], rows(v, b))
        for h in range(1, H):
            nc.sync.dma_start(q_head[h][:], rows(q, h))
            nc.sync.dma_start(k_head[h][:], rows(k, h))
        nc.sync.dma_start(offsets[:], offs)
        for h in range(H):
            nc.sync.dma_start(window[h][:], rows(base, h))

        ones_row = held.tile([1, P], F32, name="ones_row")
        nc.gpsimd.memset(ones_row[:], 1.0)
        zero_column = held.tile([P, 1], F32, name="zero_column")
        nc.gpsimd.memset(zero_column[:], 0.0)
        identity = held.tile([P, P], F32, name="identity")
        make_identity(nc, identity[:])
        ones_column = held.tile([P, 1], BF16, name="ones_column")
        nc.scalar.activation(ones_column[:], zero_column[:], ACT.Exp)

        inverse = held.tile([1, H], F32, name="inverse")
        head_row = held.tile([1, 2 * H], F32, name="head_row")
        nc.vector.reciprocal(inverse[:], wd_row[:])
        nc.vector.tensor_scalar(head_row[:, H : 2 * H], inverse[:], HUGE, -HUGE, MIN, MAX)
        nc.vector.tensor_tensor(head_row[:, 0:H], wa_row[:], head_row[:, H : 2 * H], MULT)
        head_numbers = held.tile([P, 2 * H], F32, name="head_numbers")
        heads_psum = psum_small.tile([P, 2 * H], F32, name="heads_psum", tag="small")
        nc.tensor.matmul(heads_psum[:], lhsT=ones_row[:], rhs=head_row[:], start=True, stop=True)
        nc.vector.tensor_copy(head_numbers[:], heads_psum[:])
        bounded_wd = held.tile([1, H], F32, name="bounded_wd")
        scale_row = held.tile([1, H], F32, name="scale_row")
        nc.vector.reciprocal(bounded_wd[:], head_row[:, H : 2 * H])
        nc.vector.tensor_scalar_mul(scale_row[:], bounded_wd[:], 1.0 / math.sqrt(D))
        exp_scale = held.tile([P, H], F32, name="exp_scale")
        scale_psum = psum_r.tile([P, H], F32, name="scale_psum", tag="r_psum")
        nc.tensor.matmul(scale_psum[:], lhsT=ones_row[:], rhs=scale_row[:], start=True, stop=True)
        nc.scalar.copy(exp_scale[:], scale_psum[:])

        def wa_over_wd(h):
            return head_numbers[:, h : h + 1]

        def one_over_wd(h):
            return head_numbers[:, H + h : H + h + 1]

        def wd_over_root(h):
            return exp_scale[:, h : h + 1]

        blocks = [(h, b) for h in range(H) for b in range(KEY_BLOCKS)]
        modulation = {hb: held.tile([P, N], F32, name=f"modulation{hb[0]}_{hb[1]}") for hb in blocks}
        modulated = {hb: held.tile([P, N], F32, name=f"modulated{hb[0]}_{hb[1]}") for hb in blocks}
        e = {hb: held.tile([P, N], BF16, name=f"e{hb[0]}_{hb[1]}") for hb in blocks}
        u = [held.tile([P, N], F32, name=f"u{h}") for h in range(H)]
        r = [held.tile([P, N], F32, name=f"r{h}") for h in range(H)]
        s_psum, u_psum, sums_psum = {}, {}, {}

        def modulate(h, b):
            nc.vector.scalar_tensor_tensor(modulation[h, b][:], adj_block[b][:], wa_over_wd(h), dist_block[b][:], MULT, ADD)

        def scores(h, b):
            s_psum[h, b] = psum_s.tile([P, N], F32, name="s_psum")
            nc.tensor.matmul(s_psum[h, b][:], lhsT=k_head[h][:, b * P : (b + 1) * P], rhs=q_head[h][:], start=True, stop=True)

        def exponentiate(h, b):
            nc.vector.scalar_tensor_tensor(modulated[h, b][:], modulation[h, b][:], one_over_wd(h), s_psum[h, b][:], ADD, MULT)
            nc.scalar.activation(e[h, b][:], modulated[h, b][:], ACT.Exp, scale=wd_over_root(h))

        def accumulate(h, b):
            if b == 0:
                u_psum[h] = psum_u.tile([P, N], F32, name="u_psum")
            nc.tensor.matmul(u_psum[h][:], lhsT=v_block[b][:, h * D : (h + 1) * D], rhs=e[h, b][:], start=(b == 0), stop=(b == KEY_BLOCKS - 1))

        def sum_exponentials(h):
            sums_psum[h] = psum_small.tile([P, QUERY_BLOCKS], F32, name="sums_psum", tag="small")
            for c in range(QUERY_BLOCKS):
                for b in range(KEY_BLOCKS):
                    nc.tensor.matmul(sums_psum[h][:, c : c + 1], lhsT=e[h, b][:, c * P : (c + 1) * P], rhs=ones_column[:], start=(b == 0), stop=(b == KEY_BLOCKS - 1))

        def invert_sums(h):
            r_columns = work.tile([P, QUERY_BLOCKS], F32, name="r_columns")
            nc.vector.reciprocal(r_columns[:], sums_psum[h][:])
            r_psum = psum_r.tile([P, N], F32, name="r_psum")
            for c in range(QUERY_BLOCKS):
                nc.tensor.transpose(r_psum[:, c * P : (c + 1) * P], r_columns[:, c : c + 1].to_broadcast([P, P]), identity[:])
            nc.scalar.copy(r[h][:], r_psum[:])
            nc.scalar.copy(u[h][:], u_psum[h][:])

        def place(h):
            nc.vector.tensor_tensor(window[h][:].indirect(offsets[:]), u[h][:], r[h][:], MULT)
            nc.sync.dma_start(rows(out, h), window[h][:])

        for b in range(KEY_BLOCKS):
            for h in range(MODULATION_AHEAD):
                modulate(h, b)
        for b in range(KEY_BLOCKS):
            scores(0, b)
        for h in range(H):
            for b in range(KEY_BLOCKS):
                exponentiate(h, b)
                if h + 1 < H:
                    scores(h + 1, b)
                accumulate(h, b)
                if h + MODULATION_AHEAD < H:
                    modulate(h + MODULATION_AHEAD, b)
            if h >= 1:
                invert_sums(h - 1)
            sum_exponentials(h)
        invert_sums(H - 1)
        for h in range(H):
            place(h)
